import numpy as np
import ml_dtypes


def mxq(x, axis, fmt="e4m3"):
    dtype, down = {"e4m3": (ml_dtypes.float8_e4m3fn, 7), "e5m2": (ml_dtypes.float8_e5m2, 14)}[fmt]
    v = np.moveaxis(np.asarray(x, np.float32).astype(ml_dtypes.bfloat16).astype(np.float64), axis, -1)
    blocks = v.reshape(v.shape[:-1] + (-1, 32))
    amax = np.abs(blocks).max(-1, keepdims=True)
    byte = np.maximum(np.where(amax > 0, np.frexp(amax)[1] - 1 + 127, 0) - down, 1)
    scale = np.exp2(byte - 127.0)
    codes = (blocks / scale).astype(np.float32).astype(dtype).astype(np.float64)
    return np.moveaxis((codes * scale).reshape(v.shape), -1, axis)


WIDE = False


def mx_kscale(k):
    if not WIDE:
        return np.ones(k)
    levels = np.array([10, -10, 5, -5, 0])
    a = np.random.permutation(np.resize(levels, k // 512 * 4)).reshape(k // 512, 4)
    idx = np.arange(k)
    return np.exp2(a[idx // 512, idx % 128 // 32])


BF16 = ml_dtypes.bfloat16


def bf(x):
    return np.asarray(x, np.float32).astype(BF16)


def f64(x):
    return np.asarray(x).astype(np.float64)


B, S, E, N_HEAD, MP_NUM, ROTARY_DIM = 2, 2048, 512, 4, 4, 64
HEAD_DIM = E // N_HEAD
LOCAL = E // MP_NUM
ROPE_BASE = 10000.0


def rotate_every_two(x):
    x1 = x[..., 0::2]
    x2 = x[..., 1::2]
    return np.stack((-x2, x1), axis=-1).reshape(x.shape)


def rope(x, sin, cos):
    x_rot = x[..., :ROTARY_DIM]
    x_pass = x[..., ROTARY_DIM:]
    x_rot = x_rot * cos + rotate_every_two(x_rot) * sin
    return np.concatenate([x_rot, x_pass], axis=-1)


def setup_inputs():
    s = mx_kscale(E)
    return {"hidden_states": bf(np.random.standard_normal((B, S, E)) * s),
            "w_qkv": bf(np.random.standard_normal((3 * E, E)) / np.sqrt(E) / s[None, :])}


def reference(hidden_states, w_qkv):
    qkv = mxq(f64(hidden_states), 2, "e4m3") @ mxq(f64(w_qkv), 1, "e4m3").T
    qkv = qkv.reshape(B, S, MP_NUM, 3 * LOCAL)
    q = qkv[..., :LOCAL].reshape(B, S, N_HEAD, HEAD_DIM)
    v = qkv[..., LOCAL:2 * LOCAL].reshape(B, S, N_HEAD, HEAD_DIM)
    k = qkv[..., 2 * LOCAL:].reshape(B, S, N_HEAD, HEAD_DIM)
    inv_freq = 1.0 / (ROPE_BASE ** (np.arange(0, ROTARY_DIM, 2) / ROTARY_DIM))
    freqs = np.arange(S)[:, None] * inv_freq[None, :]
    sin = np.repeat(np.sin(freqs), 2, axis=-1)[None, :, None, :]
    cos = np.repeat(np.cos(freqs), 2, axis=-1)[None, :, None, :]
    q = rope(q, sin, cos)
    k = rope(k, sin, cos)
    return q.transpose(0, 2, 1, 3), k.transpose(0, 2, 1, 3), v.transpose(0, 2, 1, 3)

@@ -1,0 +1,233 @@
+import math
+from contextlib import ExitStack
+
+import concourse.mybir as mybir
+from concourse.masks import make_identity
+
+F32 = mybir.dt.float32
+BF16 = mybir.dt.bfloat16
+I32 = mybir.dt.int32
+U32 = mybir.dt.uint32
+U8 = mybir.dt.uint8
+FP8X4 = mybir.dt.float8_e4m3fn_x4
+ALU = mybir.AluOpType
+ACT = mybir.ActivationFunctionType
+
+P = 128
+BATCH, SEQ, CHANNELS = 2, 2048, 512
+HEADS, HEAD_DIM, ROTARY = 4, 128, 64
+PAIRS = ROTARY // 2
+ROPE_BASE = 10000.0
+QUERY, VALUE, KEY = 0, 1, 2
+TILES = SEQ // P
+BANK = 512
+ROTARY_BANK, PLAIN_BANK, VALUE_BANK = 0, 1, 2
+CHUNK = 4
+STAGE = 4
+ROUND_MAGIC = 12582912.0
+COARSE_STEP = 2.0**-15
+
+FLOPS = 2 * BATCH * SEQ * CHANNELS * 3 * CHANNELS
+
+
+def rotation_tables(nc, pool):
+    position_int = pool.tile([P, TILES], I32)
+    nc.gpsimd.iota(position_int[:], pattern=[[1, TILES]], base=0, channel_multiplier=TILES)
+    position = pool.tile([P, TILES], F32)
+    nc.vector.tensor_copy(out=position[:], in_=position_int[:])
+
+    turns = pool.tile([P, PAIRS, TILES], F32)
+    rest = pool.tile([P, PAIRS, TILES], F32)
+    for i in range(PAIRS):
+        frequency = ROPE_BASE ** (-i / PAIRS) / (2.0 * math.pi)
+        coarse = round(frequency / COARSE_STEP) * COARSE_STEP
+        nc.vector.tensor_scalar_mul(out=turns[:, i, :], in0=position[:], scalar1=coarse)
+        nc.scalar.mul(out=rest[:, i, :], in_=position[:], mul=frequency - coarse)
+
+    whole = pool.tile([P, PAIRS, TILES], F32)
+
+    def drop_whole_turns():
+        nc.vector.tensor_scalar(
+            out=whole[:], in0=turns[:], scalar1=ROUND_MAGIC, scalar2=ROUND_MAGIC, op0=ALU.add, op1=ALU.subtract
+        )
+        nc.vector.tensor_sub(out=turns[:], in0=turns[:], in1=whole[:])
+
+    drop_whole_turns()
+    nc.vector.tensor_add(out=turns[:], in0=turns[:], in1=rest[:])
+    drop_whole_turns()
+
+    quarter = pool.tile([P, PAIRS, TILES], F32)
+    nc.vector.scalar_tensor_tensor(
+        out=quarter[:], in0=turns[:], scalar=-1.0, in1=turns[:], op0=ALU.mult, op1=ALU.min
+    )
+    nc.vector.tensor_scalar_add(out=quarter[:], in0=quarter[:], scalar1=0.25)
+
+    sin = pool.tile([P, TILES, PAIRS], F32)
+    cos = pool.tile([P, TILES, PAIRS], F32)
+    nc.scalar.activation(out=sin[:], in_=turns[:].rearrange("p i t -> p t i"), func=ACT.Sin, scale=2.0 * math.pi)
+    nc.scalar.activation(out=cos[:], in_=quarter[:].rearrange("p i t -> p t i"), func=ACT.Sin, scale=2.0 * math.pi)
+    return cos, sin
+
+
+def tile_ttcodegenattention_pa_t_kernel(tc, hidden_states, w_qkv, out_0, out_1, out_2):
+    nc = tc.nc
+    chunks_in_batch = TILES // CHUNK
+
+    with ExitStack() as ctx:
+        const = ctx.enter_context(tc.tile_pool(name="const", bufs=1))
+        tokens_in = ctx.enter_context(tc.tile_pool(name="tokens_in", bufs=BATCH * chunks_in_batch))
+        tokens_grouped = ctx.enter_context(tc.tile_pool(name="tokens_grouped", bufs=2))
+        tokens_mx = ctx.enter_context(tc.tile_pool(name="tokens_mx", bufs=3))
+        products = ctx.enter_context(tc.tile_pool(name="products", bufs=3))
+        stage = ctx.enter_context(tc.tile_pool(name="stage", bufs=4))
+        turned_psum = ctx.enter_context(tc.psum_pool(name="turned_psum", bufs=2))
+        result_psum = ctx.enter_context(tc.psum_pool(name="result_psum", bufs=2))
+
+        identity = const.tile([P, P], F32)
+        make_identity(nc, identity[:])
+
+        warm = const.tile([P, 1], F32)
+        nc.vector.memset(warm[:], 0.0)
+        nc.scalar.activation(out=warm[:], in_=warm[:], func=ACT.Sin)
+
+        weights_in = const.tile([P, 3, HEADS, CHANNELS], BF16)
+        weights_by_kind = w_qkv.rearrange("(s c p) k -> c p s k", c=3, p=P)
+        tokens_by_partition = hidden_states.rearrange("b (p t) k -> b p t k", t=TILES)
+        chunk_list = [(b, c) for b in range(BATCH) for c in range(chunks_in_batch)]
+        raw_tokens = {}
+
+        def load_weights(kind):
+            nc.sync.dma_start(out=weights_in[:, kind, :, :], in_=weights_by_kind[kind])
+
+        def load_tokens(b, c):
+            raw = tokens_in.tile([P, CHUNK, CHANNELS], BF16, name="raw")
+            nc.sync.dma_start(out=raw[:], in_=tokens_by_partition[b][:, c * CHUNK : (c + 1) * CHUNK, :])
+            raw_tokens[(b, c)] = raw
+
+        load_weights(VALUE)
+        load_tokens(0, 0)
+        load_weights(QUERY)
+        load_weights(KEY)
+        for b, c in chunk_list[1:]:
+            load_tokens(b, c)
+
+        cos, sin = rotation_tables(nc, const)
+
+        def turn_two_rows_blocks(first, second):
+            turned = turned_psum.tile([P, 2, 2, P], F32, name="turned")
+            for a, block in enumerate((first, second)):
+                words = block.bitcast(F32)
+                for u in range(2):
+                    nc.tensor.transpose(out=turned[:, a, u, :], in_=words[:, u * P : (u + 1) * P], identity=identity[:])
+            return turned
+
+        weights_grouped = const.tile([P, 3, BANK, 4], BF16, align_bytes=64)
+        weights_codes = const.tile([P, 3, BANK], U32, align_bytes=64)
+        weights_scales = const.tile([P, 3, BANK], U8, align_bytes=64)
+        grouped_words = weights_grouped[:].bitcast(F32)
+
+        def quantise_weights(bank):
+            nc.vector.quantize_mx(
+                out=weights_codes[:, bank, :].bitcast(FP8X4),
+                scales=weights_scales[:, bank, :],
+                in_=weights_grouped[:, bank, :, :].rearrange("p n v -> p (n v)"),
+            )
+
+        for h in range(0, HEADS, 2):
+            turned = turn_two_rows_blocks(weights_in[:, VALUE, h, :], weights_in[:, VALUE, h + 1, :])
+            nc.scalar.copy(
+                out=grouped_words[:, VALUE_BANK, h * HEAD_DIM : (h + 2) * HEAD_DIM, :].rearrange(
+                    "p (a d) u -> p a d u", a=2
+                ),
+                in_=turned[:].rearrange("p a u d -> p a d u"),
+            )
+        quantise_weights(VALUE_BANK)
+
+        for slot, kind in ((0, QUERY), (HEADS, KEY)):
+            for h in range(0, HEADS, 2):
+                turned = turn_two_rows_blocks(weights_in[:, kind, h, :], weights_in[:, kind, h + 1, :])
+                for a in range(2):
+                    g = slot + h + a
+                    nc.scalar.copy(
+                        out=grouped_words[:, ROTARY_BANK : PLAIN_BANK + 1, g * ROTARY : (g + 1) * ROTARY, :],
+                        in_=turned[:, a, :, :].rearrange("p u (r d) -> p r d u", r=2),
+                    )
+        quantise_weights(PLAIN_BANK)
+        quantise_weights(ROTARY_BANK)
+
+        def quantise_tokens(b, c):
+            raw = raw_tokens[(b, c)]
+            grouped = tokens_grouped.tile([P, CHUNK, P, 4], BF16, align_bytes=64, name="grouped")
+            for a in range(0, CHUNK, 2):
+                turned = turn_two_rows_blocks(raw[:, a, :], raw[:, a + 1, :])
+                nc.scalar.copy(
+                    out=grouped[:, a : a + 2, :, :].bitcast(F32),
+                    in_=turned[:].rearrange("p a u r -> p a r u"),
+                )
+            codes = tokens_mx.tile([P, CHUNK, P], U32, align_bytes=64, name="codes")
+            scales = tokens_mx.tile([P, CHUNK, P], U8, align_bytes=64, name="scales")
+            nc.vector.quantize_mx(
+                out=codes[:].rearrange("p a r -> p (a r)").bitcast(FP8X4),
+                scales=scales[:].rearrange("p a r -> p (a r)"),
+                in_=grouped[:].rearrange("p a r v -> p (a r v)"),
+            )
+            return codes, scales
+
+        def project(codes, scales, a, bank, name):
+            result = result_psum.tile([P, BANK], F32, name=name)
+            nc.tensor.matmul_mx(
+                out=result[:],
+                lhsT=codes[:, a, :].bitcast(FP8X4),
+                lhsT_scale=scales[:, a, :],
+                rhs=weights_codes[:, bank, :].bitcast(FP8X4),
+                rhs_scale=weights_scales[:, bank, :],
+                start=True,
+                stop=True,
+            )
+            return result
+
+        out_views = [o.rearrange("b h (p t) d -> b p h t d", t=TILES) for o in (out_0, out_1, out_2)]
+
+        ready = quantise_tokens(*chunk_list[0])
+        for n, (b, c) in enumerate(chunk_list):
+            codes, scales = ready
+            if n + 1 < len(chunk_list):
+                ready = quantise_tokens(*chunk_list[n + 1])
+            if (c * CHUNK) % STAGE == 0:
+                stage_qk = stage.tile([P, 2 * HEADS, STAGE, HEAD_DIM], F32, name="stage_qk")
+                stage_v = stage.tile([P, HEADS, STAGE, HEAD_DIM], F32, name="stage_v")
+            for a in range(CHUNK):
+                t = c * CHUNK + a
+                place = t % STAGE
+
+                value = project(codes, scales, a, VALUE_BANK, "value")
+                nc.scalar.copy(out=stage_v[:, :, place, :], in_=value[:].rearrange("p (h d) -> p h d", h=HEADS))
+
+                plain = project(codes, scales, a, PLAIN_BANK, "plain")
+                nc.scalar.copy(
+                    out=stage_qk[:, :, place, ROTARY:], in_=plain[:].rearrange("p (g d) -> p g d", g=2 * HEADS)
+                )
+
+                rotary = project(codes, scales, a, ROTARY_BANK, "rotary")
+                by_pair = rotary[:].rearrange("p (g i e) -> p g i e", g=2 * HEADS, e=2)
+                sin_t = sin[:, t, :].unsqueeze(1).to_broadcast([P, 2 * HEADS, PAIRS])
+                cos_t = cos[:, t, :].unsqueeze(1).unsqueeze(3).to_broadcast([P, 2 * HEADS, PAIRS, 2])
+                with_cos = products.tile([P, 2 * HEADS, PAIRS, 2], F32, name="with_cos")
+                with_sin = products.tile([P, 2, 2 * HEADS, PAIRS], F32, name="with_sin")
+                nc.vector.tensor_tensor(out=with_cos[:], in0=by_pair, in1=cos_t, op=ALU.mult)
+                nc.vector.scalar_tensor_tensor(
+                    out=with_sin[:, 0, :, :], in0=by_pair[:, :, :, 1], scalar=-1.0, in1=sin_t, op0=ALU.mult, op1=ALU.mult
+                )
+                nc.vector.tensor_tensor(out=with_sin[:, 1, :, :], in0=by_pair[:, :, :, 0], in1=sin_t, op=ALU.mult)
+                nc.gpsimd.tensor_tensor(
+                    out=stage_qk[:, :, place, :ROTARY].rearrange("p g (i e) -> p g i e", e=2),
+                    in0=with_cos[:],
+                    in1=with_sin[:].rearrange("p e g i -> p g i e"),
+                    op=ALU.add,
+                )
+
+            if ((c + 1) * CHUNK) % STAGE == 0:
+                first = (c + 1) * CHUNK - STAGE
+                nc.sync.dma_start(out=out_views[2][b][:, :, first : first + STAGE, :], in_=stage_v[:])
+                nc.sync.dma_start(out=out_views[0][b][:, :, first : first + STAGE, :], in_=stage_qk[:, :HEADS, :, :])
+                nc.sync.dma_start(out=out_views[1][b][:, :, first : first + STAGE, :], in_=stage_qk[:, HEADS:, :, :])

@@ -23,14 +23,14 @@ TILES = SEQ // P
 BANK = 512
 ROTARY_BANK, PLAIN_BANK, VALUE_BANK = 0, 1, 2
 CHUNK = 4
-STAGE = 4
+STAGE = 8
 ROUND_MAGIC = 12582912.0
 COARSE_STEP = 2.0**-15
 
 FLOPS = 2 * BATCH * SEQ * CHANNELS * 3 * CHANNELS
 
 
-def rotation_tables(nc, pool):
+def reduced_angles(nc, pool):
     position_int = pool.tile([P, TILES], I32)
     nc.gpsimd.iota(position_int[:], pattern=[[1, TILES]], base=0, channel_multiplier=TILES)
     position = pool.tile([P, TILES], F32)
@@ -61,12 +61,13 @@ def rotation_tables(nc, pool):
         out=quarter[:], in0=turns[:], scalar=-1.0, in1=turns[:], op0=ALU.mult, op1=ALU.min
     )
     nc.vector.tensor_scalar_add(out=quarter[:], in0=quarter[:], scalar1=0.25)
+    return turns, quarter
 
-    sin = pool.tile([P, TILES, PAIRS], F32)
-    cos = pool.tile([P, TILES, PAIRS], F32)
-    nc.scalar.activation(out=sin[:], in_=turns[:].rearrange("p i t -> p t i"), func=ACT.Sin, scale=2.0 * math.pi)
-    nc.scalar.activation(out=cos[:], in_=quarter[:].rearrange("p i t -> p t i"), func=ACT.Sin, scale=2.0 * math.pi)
-    return cos, sin
+
+def sine_table(nc, pool, turns, name):
+    table = pool.tile([P, TILES, PAIRS], F32, name=name)
+    nc.scalar.activation(out=table[:], in_=turns[:].rearrange("p i t -> p t i"), func=ACT.Sin, scale=2.0 * math.pi)
+    return table
 
 
 def tile_ttcodegenattention_pa_t_kernel(tc, hidden_states, w_qkv, out_0, out_1, out_2):
@@ -79,7 +80,7 @@ def tile_ttcodegenattention_pa_t_kernel(tc, hidden_states, w_qkv, out_0, out_1, 
         tokens_grouped = ctx.enter_context(tc.tile_pool(name="tokens_grouped", bufs=2))
         tokens_mx = ctx.enter_context(tc.tile_pool(name="tokens_mx", bufs=3))
         products = ctx.enter_context(tc.tile_pool(name="products", bufs=3))
-        stage = ctx.enter_context(tc.tile_pool(name="stage", bufs=4))
+        stage = ctx.enter_context(tc.tile_pool(name="stage", bufs=2))
         turned_psum = ctx.enter_context(tc.psum_pool(name="turned_psum", bufs=2))
         result_psum = ctx.enter_context(tc.psum_pool(name="result_psum", bufs=2))
 
@@ -104,14 +105,14 @@ def tile_ttcodegenattention_pa_t_kernel(tc, hidden_states, w_qkv, out_0, out_1, 
             nc.sync.dma_start(out=raw[:], in_=tokens_by_partition[b][:, c * CHUNK : (c + 1) * CHUNK, :])
             raw_tokens[(b, c)] = raw
 
-        load_weights(VALUE)
-        load_tokens(0, 0)
         load_weights(QUERY)
         load_weights(KEY)
+        load_tokens(0, 0)
+        load_weights(VALUE)
         for b, c in chunk_list[1:]:
             load_tokens(b, c)
 
-        cos, sin = rotation_tables(nc, const)
+        sine_turns, cosine_turns = reduced_angles(nc, const)
 
         def turn_two_rows_blocks(first, second):
             turned = turned_psum.tile([P, 2, 2, P], F32, name="turned")
@@ -133,16 +134,6 @@ def tile_ttcodegenattention_pa_t_kernel(tc, hidden_states, w_qkv, out_0, out_1, 
                 in_=weights_grouped[:, bank, :, :].rearrange("p n v -> p (n v)"),
             )
 
-        for h in range(0, HEADS, 2):
-            turned = turn_two_rows_blocks(weights_in[:, VALUE, h, :], weights_in[:, VALUE, h + 1, :])
-            nc.scalar.copy(
-                out=grouped_words[:, VALUE_BANK, h * HEAD_DIM : (h + 2) * HEAD_DIM, :].rearrange(
-                    "p (a d) u -> p a d u", a=2
-                ),
-                in_=turned[:].rearrange("p a u d -> p a d u"),
-            )
-        quantise_weights(VALUE_BANK)
-
         for slot, kind in ((0, QUERY), (HEADS, KEY)):
             for h in range(0, HEADS, 2):
                 turned = turn_two_rows_blocks(weights_in[:, kind, h, :], weights_in[:, kind, h + 1, :])
@@ -152,8 +143,8 @@ def tile_ttcodegenattention_pa_t_kernel(tc, hidden_states, w_qkv, out_0, out_1, 
                         out=grouped_words[:, ROTARY_BANK : PLAIN_BANK + 1, g * ROTARY : (g + 1) * ROTARY, :],
                         in_=turned[:, a, :, :].rearrange("p u (r d) -> p r d u", r=2),
                     )
-        quantise_weights(PLAIN_BANK)
         quantise_weights(ROTARY_BANK)
+        quantise_weights(PLAIN_BANK)
 
         def quantise_tokens(b, c):
             raw = raw_tokens[(b, c)]
@@ -189,6 +180,20 @@ def tile_ttcodegenattention_pa_t_kernel(tc, hidden_states, w_qkv, out_0, out_1, 
         out_views = [o.rearrange("b h (p t) d -> b p h t d", t=TILES) for o in (out_0, out_1, out_2)]
 
         ready = quantise_tokens(*chunk_list[0])
+
+        for h in range(0, HEADS, 2):
+            turned = turn_two_rows_blocks(weights_in[:, VALUE, h, :], weights_in[:, VALUE, h + 1, :])
+            nc.scalar.copy(
+                out=grouped_words[:, VALUE_BANK, h * HEAD_DIM : (h + 2) * HEAD_DIM, :].rearrange(
+                    "p (a d) u -> p a d u", a=2
+                ),
+                in_=turned[:].rearrange("p a u d -> p a d u"),
+            )
+        quantise_weights(VALUE_BANK)
+
+        sin = sine_table(nc, const, sine_turns, "sin")
+        cos = sine_table(nc, const, cosine_turns, "cos")
+
         for n, (b, c) in enumerate(chunk_list):
             codes, scales = ready
             if n + 1 < len(chunk_list):
@@ -199,14 +204,6 @@ def tile_ttcodegenattention_pa_t_kernel(tc, hidden_states, w_qkv, out_0, out_1, 
             for a in range(CHUNK):
                 t = c * CHUNK + a
                 place = t % STAGE
-
-                value = project(codes, scales, a, VALUE_BANK, "value")
-                nc.scalar.copy(out=stage_v[:, :, place, :], in_=value[:].rearrange("p (h d) -> p h d", h=HEADS))
-
-                plain = project(codes, scales, a, PLAIN_BANK, "plain")
-                nc.scalar.copy(
-                    out=stage_qk[:, :, place, ROTARY:], in_=plain[:].rearrange("p (g d) -> p g d", g=2 * HEADS)
-                )
 
                 rotary = project(codes, scales, a, ROTARY_BANK, "rotary")
                 by_pair = rotary[:].rearrange("p (g i e) -> p g i e", g=2 * HEADS, e=2)
@@ -226,8 +223,19 @@ def tile_ttcodegenattention_pa_t_kernel(tc, hidden_states, w_qkv, out_0, out_1, 
                     op=ALU.add,
                 )
 
-            if ((c + 1) * CHUNK) % STAGE == 0:
-                first = (c + 1) * CHUNK - STAGE
-                nc.sync.dma_start(out=out_views[2][b][:, :, first : first + STAGE, :], in_=stage_v[:])
-                nc.sync.dma_start(out=out_views[0][b][:, :, first : first + STAGE, :], in_=stage_qk[:, :HEADS, :, :])
-                nc.sync.dma_start(out=out_views[1][b][:, :, first : first + STAGE, :], in_=stage_qk[:, HEADS:, :, :])
+                plain = project(codes, scales, a, PLAIN_BANK, "plain")
+                nc.scalar.copy(
+                    out=stage_qk[:, :, place, ROTARY:], in_=plain[:].rearrange("p (g d) -> p g d", g=2 * HEADS)
+                )
+
+                value = project(codes, scales, a, VALUE_BANK, "value")
+                nc.scalar.copy(out=stage_v[:, :, place, :], in_=value[:].rearrange("p (h d) -> p h d", h=HEADS))
+
+            tiles_stored = STAGE // 2 if b == 0 else STAGE
+            done = (c + 1) * CHUNK
+            if done % tiles_stored == 0:
+                rows = slice(done - tiles_stored, done)
+                places = slice((done - tiles_stored) % STAGE, (done - 1) % STAGE + 1)
+                nc.sync.dma_start(out=out_views[2][b][:, :, rows, :], in_=stage_v[:, :, places, :])
+                nc.sync.dma_start(out=out_views[0][b][:, :, rows, :], in_=stage_qk[:, :HEADS, places, :])
+                nc.sync.dma_start(out=out_views[1][b][:, :, rows, :], in_=stage_qk[:, HEADS:, places, :])

@@ -26,6 +26,8 @@ CHUNK = 4
 STAGE = 8
 ROUND_MAGIC = 12582912.0
 COARSE_STEP = 2.0**-15
+SPLIT_PAIRS = 12
+VECTOR_ADDS_EVERY = 4
 
 FLOPS = 2 * BATCH * SEQ * CHANNELS * 3 * CHANNELS
 
@@ -37,12 +39,15 @@ def reduced_angles(nc, pool):
     nc.vector.tensor_copy(out=position[:], in_=position_int[:])
 
     turns = pool.tile([P, PAIRS, TILES], F32)
-    rest = pool.tile([P, PAIRS, TILES], F32)
+    rest = pool.tile([P, SPLIT_PAIRS, TILES], F32)
     for i in range(PAIRS):
         frequency = ROPE_BASE ** (-i / PAIRS) / (2.0 * math.pi)
-        coarse = round(frequency / COARSE_STEP) * COARSE_STEP
-        nc.vector.tensor_scalar_mul(out=turns[:, i, :], in0=position[:], scalar1=coarse)
-        nc.scalar.mul(out=rest[:, i, :], in_=position[:], mul=frequency - coarse)
+        if i < SPLIT_PAIRS:
+            coarse = round(frequency / COARSE_STEP) * COARSE_STEP
+            nc.vector.tensor_scalar_mul(out=turns[:, i, :], in0=position[:], scalar1=coarse)
+            nc.scalar.mul(out=rest[:, i, :], in_=position[:], mul=frequency - coarse)
+        else:
+            nc.vector.tensor_scalar_mul(out=turns[:, i, :], in0=position[:], scalar1=frequency)
 
     whole = pool.tile([P, PAIRS, TILES], F32)
 
@@ -53,7 +58,7 @@ def reduced_angles(nc, pool):
         nc.vector.tensor_sub(out=turns[:], in0=turns[:], in1=whole[:])
 
     drop_whole_turns()
-    nc.vector.tensor_add(out=turns[:], in0=turns[:], in1=rest[:])
+    nc.vector.tensor_add(out=turns[:, :SPLIT_PAIRS, :], in0=turns[:, :SPLIT_PAIRS, :], in1=rest[:])
     drop_whole_turns()
 
     quarter = pool.tile([P, PAIRS, TILES], F32)
@@ -216,7 +221,8 @@ def tile_ttcodegenattention_pa_t_kernel(tc, hidden_states, w_qkv, out_0, out_1, 
                     out=with_sin[:, 0, :, :], in0=by_pair[:, :, :, 1], scalar=-1.0, in1=sin_t, op0=ALU.mult, op1=ALU.mult
                 )
                 nc.vector.tensor_tensor(out=with_sin[:, 1, :, :], in0=by_pair[:, :, :, 0], in1=sin_t, op=ALU.mult)
-                nc.gpsimd.tensor_tensor(
+                adder = nc.vector if t % VECTOR_ADDS_EVERY == 0 else nc.gpsimd
+                adder.tensor_tensor(
                     out=stage_qk[:, :, place, :ROTARY].rearrange("p g (i e) -> p g i e", e=2),
                     in0=with_cos[:],
                     in1=with_sin[:].rearrange("p e g i -> p g i e"),

import math
from contextlib import ExitStack

import concourse.mybir as mybir
from concourse.masks import make_identity

F32 = mybir.dt.float32
BF16 = mybir.dt.bfloat16
I32 = mybir.dt.int32
U32 = mybir.dt.uint32
U8 = mybir.dt.uint8
FP8X4 = mybir.dt.float8_e4m3fn_x4
ALU = mybir.AluOpType
ACT = mybir.ActivationFunctionType

P = 128
BATCH, SEQ, CHANNELS = 2, 2048, 512
HEADS, HEAD_DIM, ROTARY = 4, 128, 64
PAIRS = ROTARY // 2
ROPE_BASE = 10000.0
QUERY, VALUE, KEY = 0, 1, 2
TILES = SEQ // P
BANK = 512
ROTARY_BANK, PLAIN_BANK, VALUE_BANK = 0, 1, 2
CHUNK = 4
STAGE = 8
ROUND_MAGIC = 12582912.0
COARSE_STEP = 2.0**-15
SPLIT_PAIRS = 12
VECTOR_ADDS_EVERY = 4

FLOPS = 2 * BATCH * SEQ * CHANNELS * 3 * CHANNELS


def reduced_angles(nc, pool):
    position_int = pool.tile([P, TILES], I32)
    nc.gpsimd.iota(position_int[:], pattern=[[1, TILES]], base=0, channel_multiplier=TILES)
    position = pool.tile([P, TILES], F32)
    nc.vector.tensor_copy(out=position[:], in_=position_int[:])

    turns = pool.tile([P, PAIRS, TILES], F32)
    rest = pool.tile([P, SPLIT_PAIRS, TILES], F32)
    for i in range(PAIRS):
        frequency = ROPE_BASE ** (-i / PAIRS) / (2.0 * math.pi)
        if i < SPLIT_PAIRS:
            coarse = round(frequency / COARSE_STEP) * COARSE_STEP
            nc.vector.tensor_scalar_mul(out=turns[:, i, :], in0=position[:], scalar1=coarse)
            nc.scalar.mul(out=rest[:, i, :], in_=position[:], mul=frequency - coarse)
        else:
            nc.vector.tensor_scalar_mul(out=turns[:, i, :], in0=position[:], scalar1=frequency)

    whole = pool.tile([P, PAIRS, TILES], F32)

    def drop_whole_turns():
        nc.vector.tensor_scalar(
            out=whole[:], in0=turns[:], scalar1=ROUND_MAGIC, scalar2=ROUND_MAGIC, op0=ALU.add, op1=ALU.subtract
        )
        nc.vector.tensor_sub(out=turns[:], in0=turns[:], in1=whole[:])

    drop_whole_turns()
    nc.vector.tensor_add(out=turns[:, :SPLIT_PAIRS, :], in0=turns[:, :SPLIT_PAIRS, :], in1=rest[:])
    drop_whole_turns()

    quarter = pool.tile([P, PAIRS, TILES], F32)
    nc.vector.scalar_tensor_tensor(
        out=quarter[:], in0=turns[:], scalar=-1.0, in1=turns[:], op0=ALU.mult, op1=ALU.min
    )
    nc.vector.tensor_scalar_add(out=quarter[:], in0=quarter[:], scalar1=0.25)
    return turns, quarter


def sine_table(nc, pool, turns, name):
    table = pool.tile([P, TILES, PAIRS], F32, name=name)
    nc.scalar.activation(out=table[:], in_=turns[:].rearrange("p i t -> p t i"), func=ACT.Sin, scale=2.0 * math.pi)
    return table


def tile_ttcodegenattention_pa_t_kernel(tc, hidden_states, w_qkv, out_0, out_1, out_2):
    nc = tc.nc
    chunks_in_batch = TILES // CHUNK

    with ExitStack() as ctx:
        const = ctx.enter_context(tc.tile_pool(name="const", bufs=1))
        tokens_in = ctx.enter_context(tc.tile_pool(name="tokens_in", bufs=BATCH * chunks_in_batch))
        tokens_grouped = ctx.enter_context(tc.tile_pool(name="tokens_grouped", bufs=2))
        tokens_mx = ctx.enter_context(tc.tile_pool(name="tokens_mx", bufs=3))
        products = ctx.enter_context(tc.tile_pool(name="products", bufs=3))
        stage = ctx.enter_context(tc.tile_pool(name="stage", bufs=2))
        turned_psum = ctx.enter_context(tc.psum_pool(name="turned_psum", bufs=2))
        result_psum = ctx.enter_context(tc.psum_pool(name="result_psum", bufs=2))

        identity = const.tile([P, P], F32)
        make_identity(nc, identity[:])

        warm = const.tile([P, 1], F32)
        nc.vector.memset(warm[:], 0.0)
        nc.scalar.activation(out=warm[:], in_=warm[:], func=ACT.Sin)

        weights_in = const.tile([P, 3, HEADS, CHANNELS], BF16)
        weights_by_kind = w_qkv.rearrange("(s c p) k -> c p s k", c=3, p=P)
        tokens_by_partition = hidden_states.rearrange("b (p t) k -> b p t k", t=TILES)
        chunk_list = [(b, c) for b in range(BATCH) for c in range(chunks_in_batch)]
        raw_tokens = {}

        def load_weights(kind):
            nc.sync.dma_start(out=weights_in[:, kind, :, :], in_=weights_by_kind[kind])

        def load_tokens(b, c):
            raw = tokens_in.tile([P, CHUNK, CHANNELS], BF16, name="raw")
            nc.sync.dma_start(out=raw[:], in_=tokens_by_partition[b][:, c * CHUNK : (c + 1) * CHUNK, :])
            raw_tokens[(b, c)] = raw

        load_weights(QUERY)
        load_weights(KEY)
        load_tokens(0, 0)
        load_weights(VALUE)
        for b, c in chunk_list[1:]:
            load_tokens(b, c)

        sine_turns, cosine_turns = reduced_angles(nc, const)

        def turn_two_rows_blocks(first, second):
            turned = turned_psum.tile([P, 2, 2, P], F32, name="turned")
            for a, block in enumerate((first, second)):
                words = block.bitcast(F32)
                for u in range(2):
                    nc.tensor.transpose(out=turned[:, a, u, :], in_=words[:, u * P : (u + 1) * P], identity=identity[:])
            return turned

        weights_grouped = const.tile([P, 3, BANK, 4], BF16, align_bytes=64)
        weights_codes = const.tile([P, 3, BANK], U32, align_bytes=64)
        weights_scales = const.tile([P, 3, BANK], U8, align_bytes=64)
        grouped_words = weights_grouped[:].bitcast(F32)

        def quantise_weights(bank):
            nc.vector.quantize_mx(
                out=weights_codes[:, bank, :].bitcast(FP8X4),
                scales=weights_scales[:, bank, :],
                in_=weights_grouped[:, bank, :, :].rearrange("p n v -> p (n v)"),
            )

        for slot, kind in ((0, QUERY), (HEADS, KEY)):
            for h in range(0, HEADS, 2):
                turned = turn_two_rows_blocks(weights_in[:, kind, h, :], weights_in[:, kind, h + 1, :])
                for a in range(2):
                    g = slot + h + a
                    nc.scalar.copy(
                        out=grouped_words[:, ROTARY_BANK : PLAIN_BANK + 1, g * ROTARY : (g + 1) * ROTARY, :],
                        in_=turned[:, a, :, :].rearrange("p u (r d) -> p r d u", r=2),
                    )
        quantise_weights(ROTARY_BANK)
        quantise_weights(PLAIN_BANK)

        def quantise_tokens(b, c):
            raw = raw_tokens[(b, c)]
            grouped = tokens_grouped.tile([P, CHUNK, P, 4], BF16, align_bytes=64, name="grouped")
            for a in range(0, CHUNK, 2):
                turned = turn_two_rows_blocks(raw[:, a, :], raw[:, a + 1, :])
                nc.scalar.copy(
                    out=grouped[:, a : a + 2, :, :].bitcast(F32),
                    in_=turned[:].rearrange("p a u r -> p a r u"),
                )
            codes = tokens_mx.tile([P, CHUNK, P], U32, align_bytes=64, name="codes")
            scales = tokens_mx.tile([P, CHUNK, P], U8, align_bytes=64, name="scales")
            nc.vector.quantize_mx(
                out=codes[:].rearrange("p a r -> p (a r)").bitcast(FP8X4),
                scales=scales[:].rearrange("p a r -> p (a r)"),
                in_=grouped[:].rearrange("p a r v -> p (a r v)"),
            )
            return codes, scales

        def project(codes, scales, a, bank, name):
            result = result_psum.tile([P, BANK], F32, name=name)
            nc.tensor.matmul_mx(
                out=result[:],
                lhsT=codes[:, a, :].bitcast(FP8X4),
                lhsT_scale=scales[:, a, :],
                rhs=weights_codes[:, bank, :].bitcast(FP8X4),
                rhs_scale=weights_scales[:, bank, :],
                start=True,
                stop=True,
            )
            return result

        out_views = [o.rearrange("b h (p t) d -> b p h t d", t=TILES) for o in (out_0, out_1, out_2)]

        ready = quantise_tokens(*chunk_list[0])

        for h in range(0, HEADS, 2):
            turned = turn_two_rows_blocks(weights_in[:, VALUE, h, :], weights_in[:, VALUE, h + 1, :])
            nc.scalar.copy(
                out=grouped_words[:, VALUE_BANK, h * HEAD_DIM : (h + 2) * HEAD_DIM, :].rearrange(
                    "p (a d) u -> p a d u", a=2
                ),
                in_=turned[:].rearrange("p a u d -> p a d u"),
            )
        quantise_weights(VALUE_BANK)

        sin = sine_table(nc, const, sine_turns, "sin")
        cos = sine_table(nc, const, cosine_turns, "cos")

        for n, (b, c) in enumerate(chunk_list):
            codes, scales = ready
            if n + 1 < len(chunk_list):
                ready = quantise_tokens(*chunk_list[n + 1])
            if (c * CHUNK) % STAGE == 0:
                stage_qk = stage.tile([P, 2 * HEADS, STAGE, HEAD_DIM], F32, name="stage_qk")
                stage_v = stage.tile([P, HEADS, STAGE, HEAD_DIM], F32, name="stage_v")
            for a in range(CHUNK):
                t = c * CHUNK + a
                place = t % STAGE

                rotary = project(codes, scales, a, ROTARY_BANK, "rotary")
                by_pair = rotary[:].rearrange("p (g i e) -> p g i e", g=2 * HEADS, e=2)
                sin_t = sin[:, t, :].unsqueeze(1).to_broadcast([P, 2 * HEADS, PAIRS])
                cos_t = cos[:, t, :].unsqueeze(1).unsqueeze(3).to_broadcast([P, 2 * HEADS, PAIRS, 2])
                with_cos = products.tile([P, 2 * HEADS, PAIRS, 2], F32, name="with_cos")
                with_sin = products.tile([P, 2, 2 * HEADS, PAIRS], F32, name="with_sin")
                nc.vector.tensor_tensor(out=with_cos[:], in0=by_pair, in1=cos_t, op=ALU.mult)
                nc.vector.scalar_tensor_tensor(
                    out=with_sin[:, 0, :, :], in0=by_pair[:, :, :, 1], scalar=-1.0, in1=sin_t, op0=ALU.mult, op1=ALU.mult
                )
                nc.vector.tensor_tensor(out=with_sin[:, 1, :, :], in0=by_pair[:, :, :, 0], in1=sin_t, op=ALU.mult)
                adder = nc.vector if t % VECTOR_ADDS_EVERY == 0 else nc.gpsimd
                adder.tensor_tensor(
                    out=stage_qk[:, :, place, :ROTARY].rearrange("p g (i e) -> p g i e", e=2),
                    in0=with_cos[:],
                    in1=with_sin[:].rearrange("p e g i -> p g i e"),
                    op=ALU.add,
                )

                plain = project(codes, scales, a, PLAIN_BANK, "plain")
                nc.scalar.copy(
                    out=stage_qk[:, :, place, ROTARY:], in_=plain[:].rearrange("p (g d) -> p g d", g=2 * HEADS)
                )

                value = project(codes, scales, a, VALUE_BANK, "value")
                nc.scalar.copy(out=stage_v[:, :, place, :], in_=value[:].rearrange("p (h d) -> p h d", h=HEADS))

            tiles_stored = STAGE // 2 if b == 0 else STAGE
            done = (c + 1) * CHUNK
            if done % tiles_stored == 0:
                rows = slice(done - tiles_stored, done)
                places = slice((done - tiles_stored) % STAGE, (done - 1) % STAGE + 1)
                nc.sync.dma_start(out=out_views[2][b][:, :, rows, :], in_=stage_v[:, :, places, :])
                nc.sync.dma_start(out=out_views[0][b][:, :, rows, :], in_=stage_qk[:, :HEADS, places, :])
                nc.sync.dma_start(out=out_views[1][b][:, :, rows, :], in_=stage_qk[:, HEADS:, places, :])
